import numpy as np
import ml_dtypes


def mxq(x, axis, fmt="e4m3"):
    dtype, down = {"e4m3": (ml_dtypes.float8_e4m3fn, 7), "e5m2": (ml_dtypes.float8_e5m2, 14)}[fmt]
    v = np.moveaxis(np.asarray(x, np.float32).astype(ml_dtypes.bfloat16).astype(np.float64), axis, -1)
    blocks = v.reshape(v.shape[:-1] + (-1, 32))
    amax = np.abs(blocks).max(-1, keepdims=True)
    byte = np.maximum(np.where(amax > 0, np.frexp(amax)[1] - 1 + 127, 0) - down, 1)
    scale = np.exp2(byte - 127.0)
    codes = (blocks / scale).astype(np.float32).astype(dtype).astype(np.float64)
    return np.moveaxis((codes * scale).reshape(v.shape), -1, axis)


WIDE = False


def mx_kscale(k):
    if not WIDE:
        return np.ones(k)
    levels = np.array([10, -10, 5, -5, 0])
    a = np.random.permutation(np.resize(levels, k // 512 * 4)).reshape(k // 512, 4)
    idx = np.arange(k)
    return np.exp2(a[idx // 512, idx % 128 // 32])


BF16 = ml_dtypes.bfloat16


def bf(x):
    return np.asarray(x, np.float32).astype(BF16)


def f64(x):
    return np.asarray(x).astype(np.float64)


B, S, D, NH, NKV, HD, QB = 1, 128, 512, 16, 4, 128, 512
Q_DIM = NH * HD
KV_DIM = NKV * HD


def rot(t, f0, f1):
    tp = t.reshape(t.shape[:-1] + (HD // 2, 2))
    t0, t1 = tp[..., 0], tp[..., 1]
    row1 = t0 * f0 + t1 * f1
    row0 = t0 * f1 - t1 * f0
    return np.stack([row0, row1], axis=-1).reshape(t.shape)


def setup_inputs():
    s = mx_kscale(D)
    return {"x": bf(np.random.standard_normal((B, S, D)) * s),
            "freqs_cis": bf(np.random.standard_normal((S, HD))),
            "Wqkv": bf(np.random.standard_normal((Q_DIM + 2 * KV_DIM, D)) / np.sqrt(D) / s)}


def reference(x, freqs_cis, Wqkv):
    xqkv = mxq(f64(x), 2, "e4m3") @ mxq(f64(Wqkv), 1, "e4m3").T
    xq = xqkv[..., :Q_DIM].reshape(B, S, NH, HD)
    xk = xqkv[..., Q_DIM:Q_DIM + KV_DIM].reshape(B, S, NKV, HD)
    xv = xqkv[..., Q_DIM + KV_DIM:].reshape(B, S, NKV, HD)
    f = f64(freqs_cis).reshape(S, 1, HD // 2, 2)
    f0, f1 = f[..., 0], f[..., 1]
    q_rot = rot(xq, f0, f1).transpose(0, 2, 1, 3)
    k_rot = rot(xk, f0, f1).transpose(0, 2, 1, 3)
    v = xv.transpose(0, 2, 1, 3)
    return q_rot, k_rot, v

@@ -1,0 +1,158 @@
+from contextlib import ExitStack
+
+import concourse.mybir as mybir
+from concourse.masks import make_identity
+
+BF16 = mybir.dt.bfloat16
+F32 = mybir.dt.float32
+U32 = mybir.dt.uint32
+U8 = mybir.dt.uint8
+FP8X4 = mybir.dt.float8_e4m3fn_x4
+MULT = mybir.AluOpType.mult
+ADD = mybir.AluOpType.add
+
+P = 128
+D = 512
+HD = 128
+PAIRS = HD // 2
+N_Q_HEADS = 16
+N_KV_HEADS = 4
+CHUNK = 512
+CHUNK_HEADS = CHUNK // HD
+ROWS = CHUNK // P
+N_CHUNKS = (N_Q_HEADS + 2 * N_KV_HEADS) // CHUNK_HEADS
+N_ROTATED = (N_Q_HEADS + N_KV_HEADS) // CHUNK_HEADS
+WORDS = D // 2
+HALF = CHUNK // 2
+
+FLOPS = 2 * P * D * (N_Q_HEADS + 2 * N_KV_HEADS) * HD
+
+
+def tile_rlaattention_pa_s_kernel(tc, x, freqs_cis, Wqkv, out_0, out_1, out_2):
+    nc = tc.nc
+    with ExitStack() as ctx:
+        const = ctx.enter_context(tc.tile_pool(name="const", bufs=1))
+        weights = ctx.enter_context(tc.tile_pool(name="weights", bufs=N_CHUNKS))
+        stage = ctx.enter_context(tc.tile_pool(name="stage", bufs=3))
+        flipped = ctx.enter_context(tc.psum_pool(name="flipped", bufs=4))
+        sums = ctx.enter_context(tc.psum_pool(name="sums", bufs=3))
+
+        x_sb = const.tile([P, D], BF16)
+        nc.sync.dma_start(out=x_sb[:], in_=x.flatten_outer_dims())
+        w_rows = Wqkv.rearrange("(c p b) k -> c p (b k)", p=P, b=ROWS)
+        freqs = const.tile([P, PAIRS, 2], BF16)
+        w_sb = []
+        for c in range(N_CHUNKS):
+            w_c = weights.tile([P, ROWS * D], BF16, tag="w", name="w%d" % c)
+            nc.sync.dma_start(out=w_c[:], in_=w_rows[c])
+            w_sb.append(w_c)
+            if c == 0:
+                nc.sync.dma_start(
+                    out=freqs[:], in_=freqs_cis.rearrange("s (j e) -> s j e", e=2)
+                )
+
+        ident = const.tile([P, P], F32)
+        make_identity(nc, ident[:])
+
+        x_words = x_sb[:].bitcast(F32)
+        x_flip = flipped.tile([P, 2, P], F32, tag="bank")
+        for u in range(2):
+            nc.tensor.transpose(x_flip[:, u, :], x_words[:, u * P : (u + 1) * P], ident[:])
+        x_grouped = const.tile([P, 4 * P], BF16, align_bytes=64)
+        nc.vector.tensor_copy(
+            out=x_grouped[:].bitcast(F32).rearrange("q (s u) -> q s u", u=2),
+            in_=x_flip[:].rearrange("q u s -> q s u"),
+        )
+        x_codes = const.tile([P, P], U32, align_bytes=64)
+        x_scales = const.tile([P, P], U8, align_bytes=64)
+        nc.vector.quantize_mx(
+            out=x_codes[:].bitcast(FP8X4), scales=x_scales[:], in_=x_grouped[:]
+        )
+
+        table = const.tile([P, 2, PAIRS, 2], F32)
+        nc.vector.tensor_copy(out=table[:, 0, :, 0], in_=freqs[:, :, 1])
+        nc.vector.tensor_copy(out=table[:, 0, :, 1], in_=freqs[:, :, 0])
+        nc.vector.tensor_scalar_mul(out=table[:, 1, :, 0], in0=freqs[:, :, 0], scalar1=-1.0)
+        nc.vector.tensor_copy(out=table[:, 1, :, 1], in_=freqs[:, :, 1])
+
+        head_views = [
+            out_0.rearrange("b h s f -> s (b h) f"),
+            out_1.rearrange("b h s f -> s (b h) f"),
+            out_2.rearrange("b h s f -> s (b h) f"),
+        ]
+
+        def quantise_chunk(c):
+            w_words = w_sb[c][:].bitcast(F32)
+            grouped = stage.tile([P, 4 * CHUNK], BF16, align_bytes=64)
+            grouped_words = grouped[:].bitcast(F32).rearrange(
+                "q (e p w) -> q e p w", e=2, p=P
+            )
+            for e in range(2):
+                bank = flipped.tile([P, 2, 2, P], F32, tag="bank")
+                for b2 in range(2):
+                    for u in range(2):
+                        first = ((2 * b2 + e) * 2 + u) * P
+                        nc.tensor.transpose(
+                            bank[:, b2, u, :], w_words[:, first : first + P], ident[:]
+                        )
+                nc.scalar.copy(
+                    out=grouped_words[:, e, :, :],
+                    in_=bank[:].rearrange("q b u p -> q p (b u)"),
+                )
+            codes = stage.tile([P, CHUNK], U32, align_bytes=64)
+            scales = stage.tile([P, CHUNK], U8, align_bytes=64)
+            nc.vector.quantize_mx(
+                out=codes[:].bitcast(FP8X4), scales=scales[:], in_=grouped[:]
+            )
+            return codes, scales
+
+        def project_chunk(c, codes, scales):
+            acc = sums.tile([P, CHUNK], F32)
+            nc.tensor.matmul_mx(
+                out=acc[:],
+                lhsT=x_codes[:].bitcast(FP8X4),
+                lhsT_scale=x_scales[:],
+                rhs=codes[:].bitcast(FP8X4),
+                rhs_scale=scales[:],
+                start=True,
+                stop=True,
+            )
+            result = stage.tile([P, CHUNK], F32)
+            if c < N_ROTATED:
+                shape = [P, 2, CHUNK_HEADS, PAIRS, 2]
+                products = stage.tile([P, 2, CHUNK], F32)
+                nc.vector.tensor_tensor(
+                    out=products[:].rearrange(
+                        "s e (h j r) -> s e h j r", h=CHUNK_HEADS, r=2
+                    ),
+                    in0=acc[:]
+                    .rearrange("s (e h j) -> s e h j", e=2, h=CHUNK_HEADS)
+                    .unsqueeze(4)
+                    .to_broadcast(shape),
+                    in1=table[:].unsqueeze(2).to_broadcast(shape),
+                    op=MULT,
+                )
+                nc.vector.tensor_tensor(
+                    out=result[:], in0=products[:, 0, :], in1=products[:, 1, :], op=ADD
+                )
+            else:
+                nc.scalar.copy(
+                    out=result[:].rearrange("s (m e) -> s m e", e=2),
+                    in_=acc[:].rearrange("s (e m) -> s m e", e=2),
+                )
+            first_head = c * CHUNK_HEADS
+            if first_head < N_Q_HEADS:
+                heads = head_views[0][:, first_head : first_head + CHUNK_HEADS, :]
+            elif first_head < N_Q_HEADS + N_KV_HEADS:
+                heads = head_views[1]
+            else:
+                heads = head_views[2]
+            nc.sync.dma_start(
+                out=heads, in_=result[:].rearrange("s (h f) -> s h f", h=CHUNK_HEADS)
+            )
+
+        ready = quantise_chunk(0)
+        for c in range(N_CHUNKS):
+            ahead = quantise_chunk(c + 1) if c + 1 < N_CHUNKS else None
+            project_chunk(c, ready[0], ready[1])
+            ready = ahead

@@ -132,7 +132,7 @@ def tile_rlaattention_pa_s_kernel(tc, x, freqs_cis, Wqkv, out_0, out_1, out_2):
                     in1=table[:].unsqueeze(2).to_broadcast(shape),
                     op=MULT,
                 )
-                nc.vector.tensor_tensor(
+                nc.gpsimd.tensor_tensor(
                     out=result[:], in0=products[:, 0, :], in1=products[:, 1, :], op=ADD
                 )
             else:

@@ -10,6 +10,7 @@ U8 = mybir.dt.uint8
 FP8X4 = mybir.dt.float8_e4m3fn_x4
 MULT = mybir.AluOpType.mult
 ADD = mybir.AluOpType.add
+SUBTRACT = mybir.AluOpType.subtract
 
 P = 128
 D = 512
@@ -34,8 +35,9 @@ def tile_rlaattention_pa_s_kernel(tc, x, freqs_cis, Wqkv, out_0, out_1, out_2):
         const = ctx.enter_context(tc.tile_pool(name="const", bufs=1))
         weights = ctx.enter_context(tc.tile_pool(name="weights", bufs=N_CHUNKS))
         stage = ctx.enter_context(tc.tile_pool(name="stage", bufs=3))
+        results = ctx.enter_context(tc.tile_pool(name="results", bufs=N_CHUNKS))
         flipped = ctx.enter_context(tc.psum_pool(name="flipped", bufs=4))
-        sums = ctx.enter_context(tc.psum_pool(name="sums", bufs=3))
+        sums = ctx.enter_context(tc.psum_pool(name="sums", bufs=2))
 
         x_sb = const.tile([P, D], BF16)
         nc.sync.dma_start(out=x_sb[:], in_=x.flatten_outer_dims())
@@ -69,11 +71,14 @@ def tile_rlaattention_pa_s_kernel(tc, x, freqs_cis, Wqkv, out_0, out_1, out_2):
             out=x_codes[:].bitcast(FP8X4), scales=x_scales[:], in_=x_grouped[:]
         )
 
-        table = const.tile([P, 2, PAIRS, 2], F32)
-        nc.vector.tensor_copy(out=table[:, 0, :, 0], in_=freqs[:, :, 1])
-        nc.vector.tensor_copy(out=table[:, 0, :, 1], in_=freqs[:, :, 0])
-        nc.vector.tensor_scalar_mul(out=table[:, 1, :, 0], in0=freqs[:, :, 0], scalar1=-1.0)
-        nc.vector.tensor_copy(out=table[:, 1, :, 1], in_=freqs[:, :, 1])
+        table = const.tile([P, PAIRS, 2], F32)
+        nc.vector.scalar_tensor_tensor(
+            out=table[:, :, 0], in0=freqs[:, :, 0], scalar=-1.0, in1=freqs[:, :, 1],
+            op0=MULT, op1=SUBTRACT,
+        )
+        nc.vector.tensor_tensor(
+            out=table[:, :, 1], in0=freqs[:, :, 0], in1=freqs[:, :, 1], op=SUBTRACT
+        )
 
         head_views = [
             out_0.rearrange("b h s f -> s (b h) f"),
@@ -91,7 +96,8 @@ def tile_rlaattention_pa_s_kernel(tc, x, freqs_cis, Wqkv, out_0, out_1, out_2):
                 bank = flipped.tile([P, 2, 2, P], F32, tag="bank")
                 for b2 in range(2):
                     for u in range(2):
-                        first = ((2 * b2 + e) * 2 + u) * P
+                        row = 2 * b2 + (1 - e if c < N_ROTATED else e)
+                        first = (row * 2 + u) * P
                         nc.tensor.transpose(
                             bank[:, b2, u, :], w_words[:, first : first + P], ident[:]
                         )
@@ -117,23 +123,40 @@ def tile_rlaattention_pa_s_kernel(tc, x, freqs_cis, Wqkv, out_0, out_1, out_2):
                 start=True,
                 stop=True,
             )
-            result = stage.tile([P, CHUNK], F32)
+            result = results.tile([P, CHUNK], F32)
             if c < N_ROTATED:
-                shape = [P, 2, CHUNK_HEADS, PAIRS, 2]
-                products = stage.tile([P, 2, CHUNK], F32)
+                both = sums.tile([P, HALF], F32)
+                for r in range(2):
+                    half = slice(r * HALF, (r + 1) * HALF)
+                    nc.tensor.matmul_mx(
+                        out=both[:],
+                        lhsT=x_codes[:].bitcast(FP8X4),
+                        lhsT_scale=x_scales[:],
+                        rhs=codes[:, half].bitcast(FP8X4),
+                        rhs_scale=scales[:, half],
+                        start=(r == 0),
+                        stop=(r == 1),
+                    )
+                shape = [P, CHUNK_HEADS, PAIRS, 2]
+                products = stage.tile([P, CHUNK], F32)
                 nc.vector.tensor_tensor(
-                    out=products[:].rearrange(
-                        "s e (h j r) -> s e h j r", h=CHUNK_HEADS, r=2
-                    ),
-                    in0=acc[:]
-                    .rearrange("s (e h j) -> s e h j", e=2, h=CHUNK_HEADS)
-                    .unsqueeze(4)
-                    .to_broadcast(shape),
-                    in1=table[:].unsqueeze(2).to_broadcast(shape),
+                    out=products[:].rearrange("s (h j r) -> s h j r", h=CHUNK_HEADS, r=2),
+                    in0=acc[:].rearrange("s (r h j) -> s h j r", r=2, h=CHUNK_HEADS),
+                    in1=table[:].unsqueeze(1).to_broadcast(shape),
+                    op=MULT,
+                )
+                shared = stage.tile([P, HALF], F32)
+                nc.vector.tensor_tensor(
+                    out=shared[:].rearrange("s (h j) -> s h j", h=CHUNK_HEADS),
+                    in0=both[:].rearrange("s (h j) -> s h j", h=CHUNK_HEADS),
+                    in1=freqs[:, :, 1].unsqueeze(1).to_broadcast([P, CHUNK_HEADS, PAIRS]),
                     op=MULT,
                 )
                 nc.gpsimd.tensor_tensor(
-                    out=result[:], in0=products[:, 0, :], in1=products[:, 1, :], op=ADD
+                    out=result[:].rearrange("s (m r) -> s m r", r=2),
+                    in0=products[:].rearrange("s (m r) -> s m r", r=2),
+                    in1=shared[:].unsqueeze(2).to_broadcast([P, HALF, 2]),
+                    op=ADD,
                 )
             else:
                 nc.scalar.copy(

@@ -18,13 +18,10 @@ HD = 128
 PAIRS = HD // 2
 N_Q_HEADS = 16
 N_KV_HEADS = 4
-CHUNK = 512
-CHUNK_HEADS = CHUNK // HD
-ROWS = CHUNK // P
-N_CHUNKS = (N_Q_HEADS + 2 * N_KV_HEADS) // CHUNK_HEADS
-N_ROTATED = (N_Q_HEADS + N_KV_HEADS) // CHUNK_HEADS
-WORDS = D // 2
-HALF = CHUNK // 2
+N_ROTATED = N_Q_HEADS + N_KV_HEADS
+UNITS = (2, 2, 4, 4, 4, 2, 2, 4)
+WARM_COLUMNS = 128
+WARM_PASSES = 12
 
 FLOPS = 2 * P * D * (N_Q_HEADS + 2 * N_KV_HEADS) * HD
 
@@ -33,52 +30,82 @@ def tile_rlaattention_pa_s_kernel(tc, x, freqs_cis, Wqkv, out_0, out_1, out_2):
     nc = tc.nc
     with ExitStack() as ctx:
         const = ctx.enter_context(tc.tile_pool(name="const", bufs=1))
-        weights = ctx.enter_context(tc.tile_pool(name="weights", bufs=N_CHUNKS))
+        weights = ctx.enter_context(tc.tile_pool(name="weights", bufs=len(UNITS)))
         stage = ctx.enter_context(tc.tile_pool(name="stage", bufs=3))
-        results = ctx.enter_context(tc.tile_pool(name="results", bufs=N_CHUNKS))
+        results = ctx.enter_context(tc.tile_pool(name="results", bufs=len(UNITS)))
         flipped = ctx.enter_context(tc.psum_pool(name="flipped", bufs=4))
         sums = ctx.enter_context(tc.psum_pool(name="sums", bufs=2))
 
         x_sb = const.tile([P, D], BF16)
-        nc.sync.dma_start(out=x_sb[:], in_=x.flatten_outer_dims())
-        w_rows = Wqkv.rearrange("(c p b) k -> c p (b k)", p=P, b=ROWS)
         freqs = const.tile([P, PAIRS, 2], BF16)
         w_sb = []
-        for c in range(N_CHUNKS):
-            w_c = weights.tile([P, ROWS * D], BF16, tag="w", name="w%d" % c)
-            nc.sync.dma_start(out=w_c[:], in_=w_rows[c])
-            w_sb.append(w_c)
-            if c == 0:
+        head = 0
+        for i, n_heads in enumerate(UNITS):
+            w_i = weights.tile([P, n_heads * D], BF16, tag="w", name="w%d" % i)
+            nc.sync.dma_start(
+                out=w_i[:],
+                in_=Wqkv[head * HD : (head + n_heads) * HD, :].rearrange(
+                    "(p b) k -> p (b k)", p=P
+                ),
+            )
+            w_sb.append(w_i)
+            head += n_heads
+            if i == 0:
+                nc.sync.dma_start(out=x_sb[:], in_=x.flatten_outer_dims())
+            if i == 1:
                 nc.sync.dma_start(
                     out=freqs[:], in_=freqs_cis.rearrange("s (j e) -> s j e", e=2)
                 )
 
+        zeros = const.tile([P, 4 * WARM_COLUMNS], BF16, align_bytes=64)
+        nc.vector.memset(zeros[:].bitcast(U32), 0)
+        zero_codes = const.tile([P, WARM_COLUMNS], U32, align_bytes=64)
+        zero_scales = const.tile([P, WARM_COLUMNS], U8, align_bytes=64)
+        nc.vector.quantize_mx(
+            out=zero_codes[:].bitcast(FP8X4), scales=zero_scales[:], in_=zeros[:]
+        )
+        warm = sums.tile([P, WARM_COLUMNS], F32, tag="acc", name="warm")
+        for w in range(WARM_PASSES):
+            nc.tensor.matmul_mx(
+                out=warm[:],
+                lhsT=zero_codes[:, 0:P].bitcast(FP8X4),
+                lhsT_scale=zero_scales[:, 0:P],
+                rhs=zero_codes[:].bitcast(FP8X4),
+                rhs_scale=zero_scales[:],
+                start=True,
+                stop=True,
+            )
+
         ident = const.tile([P, P], F32)
         make_identity(nc, ident[:])
 
-        x_words = x_sb[:].bitcast(F32)
-        x_flip = flipped.tile([P, 2, P], F32, tag="bank")
-        for u in range(2):
-            nc.tensor.transpose(x_flip[:, u, :], x_words[:, u * P : (u + 1) * P], ident[:])
-        x_grouped = const.tile([P, 4 * P], BF16, align_bytes=64)
-        nc.vector.tensor_copy(
-            out=x_grouped[:].bitcast(F32).rearrange("q (s u) -> q s u", u=2),
-            in_=x_flip[:].rearrange("q u s -> q s u"),
-        )
+        table = const.tile([P, PAIRS, 2], F32)
+
+        def make_table():
+            nc.vector.scalar_tensor_tensor(
+                out=table[:, :, 0], in0=freqs[:, :, 0], scalar=-1.0, in1=freqs[:, :, 1],
+                op0=MULT, op1=SUBTRACT,
+            )
+            nc.vector.tensor_tensor(
+                out=table[:, :, 1], in0=freqs[:, :, 0], in1=freqs[:, :, 1], op=SUBTRACT
+            )
+
         x_codes = const.tile([P, P], U32, align_bytes=64)
         x_scales = const.tile([P, P], U8, align_bytes=64)
-        nc.vector.quantize_mx(
-            out=x_codes[:].bitcast(FP8X4), scales=x_scales[:], in_=x_grouped[:]
-        )
 
-        table = const.tile([P, PAIRS, 2], F32)
-        nc.vector.scalar_tensor_tensor(
-            out=table[:, :, 0], in0=freqs[:, :, 0], scalar=-1.0, in1=freqs[:, :, 1],
-            op0=MULT, op1=SUBTRACT,
-        )
-        nc.vector.tensor_tensor(
-            out=table[:, :, 1], in0=freqs[:, :, 0], in1=freqs[:, :, 1], op=SUBTRACT
-        )
+        def quantise_x():
+            x_words = x_sb[:].bitcast(F32)
+            x_flip = flipped.tile([P, 2, P], F32, tag="bank")
+            for u in range(2):
+                nc.tensor.transpose(x_flip[:, u, :], x_words[:, u * P : (u + 1) * P], ident[:])
+            x_grouped = const.tile([P, 4 * P], BF16, align_bytes=64)
+            nc.vector.tensor_copy(
+                out=x_grouped[:].bitcast(F32).rearrange("q (s u) -> q s u", u=2),
+                in_=x_flip[:].rearrange("q u s -> q s u"),
+            )
+            nc.vector.quantize_mx(
+                out=x_codes[:].bitcast(FP8X4), scales=x_scales[:], in_=x_grouped[:]
+            )
 
         head_views = [
             out_0.rearrange("b h s f -> s (b h) f"),
@@ -86,76 +113,78 @@ def tile_rlaattention_pa_s_kernel(tc, x, freqs_cis, Wqkv, out_0, out_1, out_2):
             out_2.rearrange("b h s f -> s (b h) f"),
         ]
 
-        def quantise_chunk(c):
-            w_words = w_sb[c][:].bitcast(F32)
-            grouped = stage.tile([P, 4 * CHUNK], BF16, align_bytes=64)
+        def quantise_unit(i, first_head):
+            n_heads = UNITS[i]
+            width = n_heads * HD
+            per_slot = n_heads // 2
+            w_words = w_sb[i][:].bitcast(F32)
+            grouped = stage.tile([P, 4 * width], BF16, align_bytes=64, tag="grouped", name="grouped%d" % i)
             grouped_words = grouped[:].bitcast(F32).rearrange(
                 "q (e p w) -> q e p w", e=2, p=P
             )
-            for e in range(2):
-                bank = flipped.tile([P, 2, 2, P], F32, tag="bank")
-                for b2 in range(2):
-                    for u in range(2):
-                        row = 2 * b2 + (1 - e if c < N_ROTATED else e)
-                        first = (row * 2 + u) * P
-                        nc.tensor.transpose(
-                            bank[:, b2, u, :], w_words[:, first : first + P], ident[:]
-                        )
+            for e0 in range(0, 2, 2 // per_slot):
+                slots = range(e0, e0 + 2 // per_slot)
+                bank = flipped.tile([P, len(slots), per_slot, 2, P], F32, tag="bank", name="bank")
+                for e in slots:
+                    for b in range(per_slot):
+                        row = 2 * b + (1 - e if first_head < N_ROTATED else e)
+                        for u in range(2):
+                            word = (row * 2 + u) * P
+                            nc.tensor.transpose(
+                                bank[:, e - e0, b, u, :], w_words[:, word : word + P], ident[:]
+                            )
                 nc.scalar.copy(
-                    out=grouped_words[:, e, :, :],
-                    in_=bank[:].rearrange("q b u p -> q p (b u)"),
+                    out=grouped_words[:, e0 : e0 + len(slots), :, :],
+                    in_=bank[:].rearrange("q e b u p -> q e p (b u)"),
                 )
-            codes = stage.tile([P, CHUNK], U32, align_bytes=64)
-            scales = stage.tile([P, CHUNK], U8, align_bytes=64)
+            codes = stage.tile([P, width], U32, align_bytes=64, tag="codes", name="codes%d" % i)
+            scales = stage.tile([P, width], U8, align_bytes=64, tag="scales", name="scales%d" % i)
             nc.vector.quantize_mx(
                 out=codes[:].bitcast(FP8X4), scales=scales[:], in_=grouped[:]
             )
             return codes, scales
 
-        def project_chunk(c, codes, scales):
-            acc = sums.tile([P, CHUNK], F32)
-            nc.tensor.matmul_mx(
-                out=acc[:],
-                lhsT=x_codes[:].bitcast(FP8X4),
-                lhsT_scale=x_scales[:],
-                rhs=codes[:].bitcast(FP8X4),
-                rhs_scale=scales[:],
-                start=True,
-                stop=True,
-            )
-            result = results.tile([P, CHUNK], F32)
-            if c < N_ROTATED:
-                both = sums.tile([P, HALF], F32)
-                for r in range(2):
-                    half = slice(r * HALF, (r + 1) * HALF)
-                    nc.tensor.matmul_mx(
-                        out=both[:],
-                        lhsT=x_codes[:].bitcast(FP8X4),
-                        lhsT_scale=x_scales[:],
-                        rhs=codes[:, half].bitcast(FP8X4),
-                        rhs_scale=scales[:, half],
-                        start=(r == 0),
-                        stop=(r == 1),
-                    )
-                shape = [P, CHUNK_HEADS, PAIRS, 2]
-                products = stage.tile([P, CHUNK], F32)
+        def project_unit(i, first_head, codes, scales):
+            n_heads = UNITS[i]
+            width = n_heads * HD
+            half_width = width // 2
+
+            def multiply(out, columns, start, stop):
+                nc.tensor.matmul_mx(
+                    out=out,
+                    lhsT=x_codes[:].bitcast(FP8X4),
+                    lhsT_scale=x_scales[:],
+                    rhs=codes[:, columns].bitcast(FP8X4),
+                    rhs_scale=scales[:, columns],
+                    start=start,
+                    stop=stop,
+                )
+
+            acc = sums.tile([P, width], F32, tag="acc", name="acc%d" % i)
+            multiply(acc[:], slice(0, width), True, True)
+            result = results.tile([P, width], F32, tag="result", name="result%d" % i)
+            if first_head < N_ROTATED:
+                both = sums.tile([P, half_width], F32, tag="both", name="both%d" % i)
+                multiply(both[:], slice(0, half_width), True, False)
+                multiply(both[:], slice(half_width, width), False, True)
+                products = stage.tile([P, width], F32, tag="products", name="products%d" % i)
                 nc.vector.tensor_tensor(
-                    out=products[:].rearrange("s (h j r) -> s h j r", h=CHUNK_HEADS, r=2),
-                    in0=acc[:].rearrange("s (r h j) -> s h j r", r=2, h=CHUNK_HEADS),
-                    in1=table[:].unsqueeze(1).to_broadcast(shape),
+                    out=products[:].rearrange("s (h j r) -> s h j r", h=n_heads, r=2),
+                    in0=acc[:].rearrange("s (r h j) -> s h j r", r=2, h=n_heads),
+                    in1=table[:].unsqueeze(1).to_broadcast([P, n_heads, PAIRS, 2]),
                     op=MULT,
                 )
-                shared = stage.tile([P, HALF], F32)
+                shared = stage.tile([P, half_width], F32, tag="shared", name="shared%d" % i)
                 nc.vector.tensor_tensor(
-                    out=shared[:].rearrange("s (h j) -> s h j", h=CHUNK_HEADS),
-                    in0=both[:].rearrange("s (h j) -> s h j", h=CHUNK_HEADS),
-                    in1=freqs[:, :, 1].unsqueeze(1).to_broadcast([P, CHUNK_HEADS, PAIRS]),
+                    out=shared[:].rearrange("s (h j) -> s h j", h=n_heads),
+                    in0=both[:].rearrange("s (h j) -> s h j", h=n_heads),
+                    in1=freqs[:, :, 1].unsqueeze(1).to_broadcast([P, n_heads, PAIRS]),
                     op=MULT,
                 )
                 nc.gpsimd.tensor_tensor(
                     out=result[:].rearrange("s (m r) -> s m r", r=2),
                     in0=products[:].rearrange("s (m r) -> s m r", r=2),
-                    in1=shared[:].unsqueeze(2).to_broadcast([P, HALF, 2]),
+                    in1=shared[:].unsqueeze(2).to_broadcast([P, half_width, 2]),
                     op=ADD,
                 )
             else:
@@ -163,19 +192,23 @@ def tile_rlaattention_pa_s_kernel(tc, x, freqs_cis, Wqkv, out_0, out_1, out_2):
                     out=result[:].rearrange("s (m e) -> s m e", e=2),
                     in_=acc[:].rearrange("s (e m) -> s m e", e=2),
                 )
-            first_head = c * CHUNK_HEADS
             if first_head < N_Q_HEADS:
-                heads = head_views[0][:, first_head : first_head + CHUNK_HEADS, :]
-            elif first_head < N_Q_HEADS + N_KV_HEADS:
-                heads = head_views[1]
+                heads = head_views[0][:, first_head : first_head + n_heads, :]
+            elif first_head < N_ROTATED:
+                k_head = first_head - N_Q_HEADS
+                heads = head_views[1][:, k_head : k_head + n_heads, :]
             else:
-                heads = head_views[2]
+                v_head = first_head - N_ROTATED
+                heads = head_views[2][:, v_head : v_head + n_heads, :]
             nc.sync.dma_start(
-                out=heads, in_=result[:].rearrange("s (h f) -> s h f", h=CHUNK_HEADS)
+                out=heads, in_=result[:].rearrange("s (h f) -> s h f", h=n_heads)
             )
 
-        ready = quantise_chunk(0)
-        for c in range(N_CHUNKS):
-            ahead = quantise_chunk(c + 1) if c + 1 < N_CHUNKS else None
-            project_chunk(c, ready[0], ready[1])
+        firsts = [sum(UNITS[:i]) for i in range(len(UNITS))]
+        ready = quantise_unit(0, firsts[0])
+        quantise_x()
+        make_table()
+        for i in range(len(UNITS)):
+            ahead = quantise_unit(i + 1, firsts[i + 1]) if i + 1 < len(UNITS) else None
+            project_unit(i, firsts[i], ready[0], ready[1])
             ready = ahead

@@ -181,12 +181,16 @@ def tile_rlaattention_pa_s_kernel(tc, x, freqs_cis, Wqkv, out_0, out_1, out_2):
                     in1=freqs[:, :, 1].unsqueeze(1).to_broadcast([P, n_heads, PAIRS]),
                     op=MULT,
                 )
-                nc.gpsimd.tensor_tensor(
-                    out=result[:].rearrange("s (m r) -> s m r", r=2),
-                    in0=products[:].rearrange("s (m r) -> s m r", r=2),
-                    in1=shared[:].unsqueeze(2).to_broadcast([P, half_width, 2]),
-                    op=ADD,
-                )
+                for engine, part in (
+                    (nc.vector, slice(0, half_width // 2)),
+                    (nc.gpsimd, slice(half_width // 2, half_width)),
+                ):
+                    engine.tensor_tensor(
+                        out=result[:].rearrange("s (m r) -> s m r", r=2)[:, part, :],
+                        in0=products[:].rearrange("s (m r) -> s m r", r=2)[:, part, :],
+                        in1=shared[:, part].unsqueeze(2).to_broadcast([P, half_width // 2, 2]),
+                        op=ADD,
+                    )
             else:
                 nc.scalar.copy(
                     out=result[:].rearrange("s (m e) -> s m e", e=2),

@@ -10,7 +10,6 @@ U8 = mybir.dt.uint8
 FP8X4 = mybir.dt.float8_e4m3fn_x4
 MULT = mybir.AluOpType.mult
 ADD = mybir.AluOpType.add
-SUBTRACT = mybir.AluOpType.subtract
 
 P = 128
 D = 512
@@ -19,9 +18,9 @@ PAIRS = HD // 2
 N_Q_HEADS = 16
 N_KV_HEADS = 4
 N_ROTATED = N_Q_HEADS + N_KV_HEADS
-UNITS = (2, 2, 4, 4, 4, 2, 2, 4)
-WARM_COLUMNS = 128
-WARM_PASSES = 12
+UNITS = (2, 2, 2, 2, 4, 4, 2, 2, 4)
+N_UNITS = len(UNITS)
+FIRST_HEAD = [sum(UNITS[:i]) for i in range(N_UNITS)]
 
 FLOPS = 2 * P * D * (N_Q_HEADS + 2 * N_KV_HEADS) * HD
 
@@ -30,189 +29,173 @@ def tile_rlaattention_pa_s_kernel(tc, x, freqs_cis, Wqkv, out_0, out_1, out_2):
     nc = tc.nc
     with ExitStack() as ctx:
         const = ctx.enter_context(tc.tile_pool(name="const", bufs=1))
-        weights = ctx.enter_context(tc.tile_pool(name="weights", bufs=len(UNITS)))
-        stage = ctx.enter_context(tc.tile_pool(name="stage", bufs=3))
-        results = ctx.enter_context(tc.tile_pool(name="results", bufs=len(UNITS)))
-        flipped = ctx.enter_context(tc.psum_pool(name="flipped", bufs=4))
-        sums = ctx.enter_context(tc.psum_pool(name="sums", bufs=2))
+        weights = ctx.enter_context(tc.tile_pool(name="weights", bufs=N_UNITS))
+        stage = ctx.enter_context(tc.tile_pool(name="stage", bufs=4))
+        results = ctx.enter_context(tc.tile_pool(name="results", bufs=N_UNITS))
+        flipped = ctx.enter_context(tc.psum_pool(name="flipped", bufs=5))
+        sums = ctx.enter_context(tc.psum_pool(name="sums", bufs=3))
 
-        x_sb = const.tile([P, D], BF16)
         freqs = const.tile([P, PAIRS, 2], BF16)
+        x_sb = const.tile([P, D], BF16)
         w_sb = []
-        head = 0
-        for i, n_heads in enumerate(UNITS):
-            w_i = weights.tile([P, n_heads * D], BF16, tag="w", name="w%d" % i)
-            nc.sync.dma_start(
-                out=w_i[:],
-                in_=Wqkv[head * HD : (head + n_heads) * HD, :].rearrange(
-                    "(p b) k -> p (b k)", p=P
-                ),
-            )
+        nc.sync.dma_start(out=freqs[:], in_=freqs_cis.rearrange("s (j e) -> s j e", e=2))
+        for i in range(N_UNITS):
+            rows = Wqkv[FIRST_HEAD[i] * HD : (FIRST_HEAD[i] + UNITS[i]) * HD, :]
+            w_i = weights.tile([P, UNITS[i] * D], BF16, tag="w", name="w%d" % i)
+            nc.sync.dma_start(out=w_i[:], in_=rows.rearrange("(p b) k -> p (b k)", p=P))
             w_sb.append(w_i)
-            head += n_heads
             if i == 0:
                 nc.sync.dma_start(out=x_sb[:], in_=x.flatten_outer_dims())
-            if i == 1:
-                nc.sync.dma_start(
-                    out=freqs[:], in_=freqs_cis.rearrange("s (j e) -> s j e", e=2)
-                )
-
-        zeros = const.tile([P, 4 * WARM_COLUMNS], BF16, align_bytes=64)
-        nc.vector.memset(zeros[:].bitcast(U32), 0)
-        zero_codes = const.tile([P, WARM_COLUMNS], U32, align_bytes=64)
-        zero_scales = const.tile([P, WARM_COLUMNS], U8, align_bytes=64)
-        nc.vector.quantize_mx(
-            out=zero_codes[:].bitcast(FP8X4), scales=zero_scales[:], in_=zeros[:]
-        )
-        warm = sums.tile([P, WARM_COLUMNS], F32, tag="acc", name="warm")
-        for w in range(WARM_PASSES):
-            nc.tensor.matmul_mx(
-                out=warm[:],
-                lhsT=zero_codes[:, 0:P].bitcast(FP8X4),
-                lhsT_scale=zero_scales[:, 0:P],
-                rhs=zero_codes[:].bitcast(FP8X4),
-                rhs_scale=zero_scales[:],
-                start=True,
-                stop=True,
-            )
 
         ident = const.tile([P, P], F32)
         make_identity(nc, ident[:])
 
-        table = const.tile([P, PAIRS, 2], F32)
+        table = const.tile([P, 2, PAIRS, 2], F32)
 
         def make_table():
-            nc.vector.scalar_tensor_tensor(
-                out=table[:, :, 0], in0=freqs[:, :, 0], scalar=-1.0, in1=freqs[:, :, 1],
-                op0=MULT, op1=SUBTRACT,
-            )
-            nc.vector.tensor_tensor(
-                out=table[:, :, 1], in0=freqs[:, :, 0], in1=freqs[:, :, 1], op=SUBTRACT
-            )
+            nc.vector.tensor_copy(out=table[:, 0, :, 0], in_=freqs[:, :, 1])
+            nc.vector.tensor_copy(out=table[:, 0, :, 1], in_=freqs[:, :, 0])
+            nc.vector.tensor_scalar_mul(out=table[:, 1, :, 0], in0=freqs[:, :, 0], scalar1=-1.0)
+            nc.vector.tensor_copy(out=table[:, 1, :, 1], in_=freqs[:, :, 1])
 
         x_codes = const.tile([P, P], U32, align_bytes=64)
         x_scales = const.tile([P, P], U8, align_bytes=64)
+        x_grouped = const.tile([P, 4 * P], BF16, align_bytes=64)
 
-        def quantise_x():
+        def transpose_x():
             x_words = x_sb[:].bitcast(F32)
-            x_flip = flipped.tile([P, 2, P], F32, tag="bank")
+            bank = flipped.tile([P, 2, P], F32, tag="bank", name="x_bank")
             for u in range(2):
-                nc.tensor.transpose(x_flip[:, u, :], x_words[:, u * P : (u + 1) * P], ident[:])
-            x_grouped = const.tile([P, 4 * P], BF16, align_bytes=64)
+                nc.tensor.transpose(bank[:, u, :], x_words[:, u * P : (u + 1) * P], ident[:])
             nc.vector.tensor_copy(
                 out=x_grouped[:].bitcast(F32).rearrange("q (s u) -> q s u", u=2),
-                in_=x_flip[:].rearrange("q u s -> q s u"),
+                in_=bank[:].rearrange("q u s -> q s u"),
             )
+
+        def quantise_x():
             nc.vector.quantize_mx(
                 out=x_codes[:].bitcast(FP8X4), scales=x_scales[:], in_=x_grouped[:]
             )
 
-        head_views = [
-            out_0.rearrange("b h s f -> s (b h) f"),
-            out_1.rearrange("b h s f -> s (b h) f"),
-            out_2.rearrange("b h s f -> s (b h) f"),
-        ]
+        head_views = [out.rearrange("b h s f -> s (b h) f") for out in (out_0, out_1, out_2)]
+        grouped, codes, scales, acc, products, result = {}, {}, {}, {}, {}, {}
 
-        def quantise_unit(i, first_head):
-            n_heads = UNITS[i]
-            width = n_heads * HD
-            per_slot = n_heads // 2
+        def transpose_unit(i):
+            per_slot = UNITS[i] // 2
             w_words = w_sb[i][:].bitcast(F32)
-            grouped = stage.tile([P, 4 * width], BF16, align_bytes=64, tag="grouped", name="grouped%d" % i)
-            grouped_words = grouped[:].bitcast(F32).rearrange(
-                "q (e p w) -> q e p w", e=2, p=P
+            grouped_i = stage.tile(
+                [P, 4 * UNITS[i] * HD], BF16, align_bytes=64, tag="grouped", name="grouped%d" % i
             )
+            grouped[i] = grouped_i
+            words = grouped_i[:].bitcast(F32).rearrange("q (e p w) -> q e p w", e=2, p=P)
             for e0 in range(0, 2, 2 // per_slot):
                 slots = range(e0, e0 + 2 // per_slot)
-                bank = flipped.tile([P, len(slots), per_slot, 2, P], F32, tag="bank", name="bank")
+                bank = flipped.tile(
+                    [P, len(slots), per_slot, 2, P], F32, tag="bank", name="bank%d_%d" % (i, e0)
+                )
                 for e in slots:
                     for b in range(per_slot):
-                        row = 2 * b + (1 - e if first_head < N_ROTATED else e)
                         for u in range(2):
-                            word = (row * 2 + u) * P
+                            word = ((2 * b + e) * 2 + u) * P
                             nc.tensor.transpose(
                                 bank[:, e - e0, b, u, :], w_words[:, word : word + P], ident[:]
                             )
                 nc.scalar.copy(
-                    out=grouped_words[:, e0 : e0 + len(slots), :, :],
+                    out=words[:, e0 : e0 + len(slots), :, :],
                     in_=bank[:].rearrange("q e b u p -> q e p (b u)"),
                 )
-            codes = stage.tile([P, width], U32, align_bytes=64, tag="codes", name="codes%d" % i)
-            scales = stage.tile([P, width], U8, align_bytes=64, tag="scales", name="scales%d" % i)
+
+        def quantise_unit(i):
+            width = UNITS[i] * HD
+            codes_i = stage.tile([P, width], U32, align_bytes=64, tag="codes", name="codes%d" % i)
+            scales_i = stage.tile([P, width], U8, align_bytes=64, tag="scales", name="scales%d" % i)
             nc.vector.quantize_mx(
-                out=codes[:].bitcast(FP8X4), scales=scales[:], in_=grouped[:]
+                out=codes_i[:].bitcast(FP8X4), scales=scales_i[:], in_=grouped[i][:]
             )
-            return codes, scales
+            codes[i], scales[i] = codes_i, scales_i
 
-        def project_unit(i, first_head, codes, scales):
+        def multiply_unit(i):
+            acc_i = sums.tile([P, UNITS[i] * HD], F32, tag="acc", name="acc%d" % i)
+            nc.tensor.matmul_mx(
+                out=acc_i[:],
+                lhsT=x_codes[:].bitcast(FP8X4),
+                lhsT_scale=x_scales[:],
+                rhs=codes[i][:].bitcast(FP8X4),
+                rhs_scale=scales[i][:],
+                start=True,
+                stop=True,
+            )
+            acc[i] = acc_i
+
+        def products_unit(i):
             n_heads = UNITS[i]
-            width = n_heads * HD
-            half_width = width // 2
+            products_i = stage.tile(
+                [P, 2, n_heads * HD], F32, tag="products", name="products%d" % i
+            )
+            shape = [P, 2, n_heads, PAIRS, 2]
+            nc.vector.tensor_tensor(
+                out=products_i[:].rearrange("s e (h j r) -> s e h j r", h=n_heads, r=2),
+                in0=acc[i][:]
+                .rearrange("s (e h j) -> s e h j", e=2, h=n_heads)
+                .unsqueeze(4)
+                .to_broadcast(shape),
+                in1=table[:].unsqueeze(2).to_broadcast(shape),
+                op=MULT,
+            )
+            products[i] = products_i
 
-            def multiply(out, columns, start, stop):
-                nc.tensor.matmul_mx(
-                    out=out,
-                    lhsT=x_codes[:].bitcast(FP8X4),
-                    lhsT_scale=x_scales[:],
-                    rhs=codes[:, columns].bitcast(FP8X4),
-                    rhs_scale=scales[:, columns],
-                    start=start,
-                    stop=stop,
-                )
+        def add_unit(i, engine):
+            result_i = results.tile([P, UNITS[i] * HD], F32, tag="result", name="result%d" % i)
+            engine.tensor_tensor(
+                out=result_i[:], in0=products[i][:, 0, :], in1=products[i][:, 1, :], op=ADD
+            )
+            result[i] = result_i
 
-            acc = sums.tile([P, width], F32, tag="acc", name="acc%d" % i)
-            multiply(acc[:], slice(0, width), True, True)
-            result = results.tile([P, width], F32, tag="result", name="result%d" % i)
-            if first_head < N_ROTATED:
-                both = sums.tile([P, half_width], F32, tag="both", name="both%d" % i)
-                multiply(both[:], slice(0, half_width), True, False)
-                multiply(both[:], slice(half_width, width), False, True)
-                products = stage.tile([P, width], F32, tag="products", name="products%d" % i)
-                nc.vector.tensor_tensor(
-                    out=products[:].rearrange("s (h j r) -> s h j r", h=n_heads, r=2),
-                    in0=acc[:].rearrange("s (r h j) -> s h j r", r=2, h=n_heads),
-                    in1=table[:].unsqueeze(1).to_broadcast([P, n_heads, PAIRS, 2]),
-                    op=MULT,
-                )
-                shared = stage.tile([P, half_width], F32, tag="shared", name="shared%d" % i)
-                nc.vector.tensor_tensor(
-                    out=shared[:].rearrange("s (h j) -> s h j", h=n_heads),
-                    in0=both[:].rearrange("s (h j) -> s h j", h=n_heads),
-                    in1=freqs[:, :, 1].unsqueeze(1).to_broadcast([P, n_heads, PAIRS]),
-                    op=MULT,
-                )
-                for engine, part in (
-                    (nc.vector, slice(0, half_width // 2)),
-                    (nc.gpsimd, slice(half_width // 2, half_width)),
-                ):
-                    engine.tensor_tensor(
-                        out=result[:].rearrange("s (m r) -> s m r", r=2)[:, part, :],
-                        in0=products[:].rearrange("s (m r) -> s m r", r=2)[:, part, :],
-                        in1=shared[:, part].unsqueeze(2).to_broadcast([P, half_width // 2, 2]),
-                        op=ADD,
-                    )
+        def copy_values(i):
+            result_i = results.tile([P, UNITS[i] * HD], F32, tag="result", name="result%d" % i)
+            nc.scalar.copy(
+                out=result_i[:].rearrange("s (m e) -> s m e", e=2),
+                in_=acc[i][:].rearrange("s (e m) -> s m e", e=2),
+            )
+            result[i] = result_i
+
+        def store_unit(i):
+            first = FIRST_HEAD[i]
+            if first < N_Q_HEADS:
+                heads = head_views[0][:, first : first + UNITS[i], :]
+            elif first < N_ROTATED:
+                heads = head_views[1][:, first - N_Q_HEADS : first - N_Q_HEADS + UNITS[i], :]
             else:
-                nc.scalar.copy(
-                    out=result[:].rearrange("s (m e) -> s m e", e=2),
-                    in_=acc[:].rearrange("s (e m) -> s m e", e=2),
-                )
-            if first_head < N_Q_HEADS:
-                heads = head_views[0][:, first_head : first_head + n_heads, :]
-            elif first_head < N_ROTATED:
-                k_head = first_head - N_Q_HEADS
-                heads = head_views[1][:, k_head : k_head + n_heads, :]
-            else:
-                v_head = first_head - N_ROTATED
-                heads = head_views[2][:, v_head : v_head + n_heads, :]
+                heads = head_views[2][:, first - N_ROTATED : first - N_ROTATED + UNITS[i], :]
             nc.sync.dma_start(
-                out=heads, in_=result[:].rearrange("s (h f) -> s h f", h=n_heads)
+                out=heads, in_=result[i][:].rearrange("s (h f) -> s h f", h=UNITS[i])
             )
 
-        firsts = [sum(UNITS[:i]) for i in range(len(UNITS))]
-        ready = quantise_unit(0, firsts[0])
-        quantise_x()
-        make_table()
-        for i in range(len(UNITS)):
-            ahead = quantise_unit(i + 1, firsts[i + 1]) if i + 1 < len(UNITS) else None
-            project_unit(i, firsts[i], ready[0], ready[1])
-            ready = ahead
+        with tc.manual_schedule():
+            make_table()
+            transpose_unit(0)
+            transpose_x()
+            quantise_x()
+            transposed, quantised, waiting = 1, 0, None
+            for i in range(N_UNITS):
+                while transposed < min(i + 2 + 1, N_UNITS):
+                    transpose_unit(transposed)
+                    transposed += 1
+                while quantised < min(i + 1 + 1, N_UNITS):
+                    quantise_unit(quantised)
+                    quantised += 1
+                multiply_unit(i)
+                if waiting is not None:
+                    add_unit(waiting, nc.vector)
+                    store_unit(waiting)
+                    waiting = None
+                if FIRST_HEAD[i] >= N_ROTATED:
+                    copy_values(i)
+                    store_unit(i)
+                else:
+                    products_unit(i)
+                    if FIRST_HEAD[i] + UNITS[i] == N_ROTATED:
+                        waiting = i
+                    else:
+                        add_unit(i, nc.gpsimd)
+                        store_unit(i)

@@ -10,6 +10,7 @@ U8 = mybir.dt.uint8
 FP8X4 = mybir.dt.float8_e4m3fn_x4
 MULT = mybir.AluOpType.mult
 ADD = mybir.AluOpType.add
+SUBTRACT = mybir.AluOpType.subtract
 
 P = 128
 D = 512
@@ -32,8 +33,8 @@ def tile_rlaattention_pa_s_kernel(tc, x, freqs_cis, Wqkv, out_0, out_1, out_2):
         weights = ctx.enter_context(tc.tile_pool(name="weights", bufs=N_UNITS))
         stage = ctx.enter_context(tc.tile_pool(name="stage", bufs=4))
         results = ctx.enter_context(tc.tile_pool(name="results", bufs=N_UNITS))
-        flipped = ctx.enter_context(tc.psum_pool(name="flipped", bufs=5))
-        sums = ctx.enter_context(tc.psum_pool(name="sums", bufs=3))
+        flipped = ctx.enter_context(tc.psum_pool(name="flipped", bufs=4))
+        sums = ctx.enter_context(tc.psum_pool(name="sums", bufs=2))
 
         freqs = const.tile([P, PAIRS, 2], BF16)
         x_sb = const.tile([P, D], BF16)
@@ -50,13 +51,16 @@ def tile_rlaattention_pa_s_kernel(tc, x, freqs_cis, Wqkv, out_0, out_1, out_2):
         ident = const.tile([P, P], F32)
         make_identity(nc, ident[:])
 
-        table = const.tile([P, 2, PAIRS, 2], F32)
+        table = const.tile([P, PAIRS, 2], F32)
 
         def make_table():
-            nc.vector.tensor_copy(out=table[:, 0, :, 0], in_=freqs[:, :, 1])
-            nc.vector.tensor_copy(out=table[:, 0, :, 1], in_=freqs[:, :, 0])
-            nc.vector.tensor_scalar_mul(out=table[:, 1, :, 0], in0=freqs[:, :, 0], scalar1=-1.0)
-            nc.vector.tensor_copy(out=table[:, 1, :, 1], in_=freqs[:, :, 1])
+            nc.vector.scalar_tensor_tensor(
+                out=table[:, :, 0], in0=freqs[:, :, 0], scalar=-1.0, in1=freqs[:, :, 1],
+                op0=MULT, op1=SUBTRACT,
+            )
+            nc.vector.tensor_tensor(
+                out=table[:, :, 1], in0=freqs[:, :, 0], in1=freqs[:, :, 1], op=SUBTRACT
+            )
 
         x_codes = const.tile([P, P], U32, align_bytes=64)
         x_scales = const.tile([P, P], U8, align_bytes=64)
@@ -78,7 +82,8 @@ def tile_rlaattention_pa_s_kernel(tc, x, freqs_cis, Wqkv, out_0, out_1, out_2):
             )
 
         head_views = [out.rearrange("b h s f -> s (b h) f") for out in (out_0, out_1, out_2)]
-        grouped, codes, scales, acc, products, result = {}, {}, {}, {}, {}, {}
+        grouped, codes, scales, acc, both = {}, {}, {}, {}, {}
+        products, shared, result = {}, {}, {}
 
         def transpose_unit(i):
             per_slot = UNITS[i] // 2
@@ -95,8 +100,9 @@ def tile_rlaattention_pa_s_kernel(tc, x, freqs_cis, Wqkv, out_0, out_1, out_2):
                 )
                 for e in slots:
                     for b in range(per_slot):
+                        row = 2 * b + (1 - e if FIRST_HEAD[i] < N_ROTATED else e)
                         for u in range(2):
-                            word = ((2 * b + e) * 2 + u) * P
+                            word = (row * 2 + u) * P
                             nc.tensor.transpose(
                                 bank[:, e - e0, b, u, :], w_words[:, word : word + P], ident[:]
                             )
@@ -115,39 +121,56 @@ def tile_rlaattention_pa_s_kernel(tc, x, freqs_cis, Wqkv, out_0, out_1, out_2):
             codes[i], scales[i] = codes_i, scales_i
 
         def multiply_unit(i):
-            acc_i = sums.tile([P, UNITS[i] * HD], F32, tag="acc", name="acc%d" % i)
-            nc.tensor.matmul_mx(
-                out=acc_i[:],
-                lhsT=x_codes[:].bitcast(FP8X4),
-                lhsT_scale=x_scales[:],
-                rhs=codes[i][:].bitcast(FP8X4),
-                rhs_scale=scales[i][:],
-                start=True,
-                stop=True,
-            )
+            half = UNITS[i] * HD // 2
+
+            def multiply(out, first, last, start, stop):
+                nc.tensor.matmul_mx(
+                    out=out,
+                    lhsT=x_codes[:].bitcast(FP8X4),
+                    lhsT_scale=x_scales[:],
+                    rhs=codes[i][:, first:last].bitcast(FP8X4),
+                    rhs_scale=scales[i][:, first:last],
+                    start=start,
+                    stop=stop,
+                )
+
+            acc_i = sums.tile([P, 2 * half], F32, tag="acc", name="acc%d" % i)
+            multiply(acc_i[:], 0, 2 * half, True, True)
             acc[i] = acc_i
+            if FIRST_HEAD[i] < N_ROTATED:
+                both_i = sums.tile([P, half], F32, tag="both", name="both%d" % i)
+                multiply(both_i[:], 0, half, True, False)
+                multiply(both_i[:], half, 2 * half, False, True)
+                both[i] = both_i
 
         def products_unit(i):
             n_heads = UNITS[i]
-            products_i = stage.tile(
-                [P, 2, n_heads * HD], F32, tag="products", name="products%d" % i
-            )
-            shape = [P, 2, n_heads, PAIRS, 2]
+            half = n_heads * HD // 2
+            products_i = stage.tile([P, 2 * half], F32, tag="products", name="products%d" % i)
             nc.vector.tensor_tensor(
-                out=products_i[:].rearrange("s e (h j r) -> s e h j r", h=n_heads, r=2),
-                in0=acc[i][:]
-                .rearrange("s (e h j) -> s e h j", e=2, h=n_heads)
-                .unsqueeze(4)
-                .to_broadcast(shape),
-                in1=table[:].unsqueeze(2).to_broadcast(shape),
+                out=products_i[:].rearrange("s (h j r) -> s h j r", h=n_heads, r=2),
+                in0=acc[i][:].rearrange("s (r h j) -> s h j r", r=2, h=n_heads),
+                in1=table[:].unsqueeze(1).to_broadcast([P, n_heads, PAIRS, 2]),
                 op=MULT,
             )
             products[i] = products_i
+            shared_i = stage.tile([P, half], F32, tag="shared", name="shared%d" % i)
+            nc.vector.tensor_tensor(
+                out=shared_i[:].rearrange("s (h j) -> s h j", h=n_heads),
+                in0=both[i][:].rearrange("s (h j) -> s h j", h=n_heads),
+                in1=freqs[:, :, 1].unsqueeze(1).to_broadcast([P, n_heads, PAIRS]),
+                op=MULT,
+            )
+            shared[i] = shared_i
 
         def add_unit(i, engine):
-            result_i = results.tile([P, UNITS[i] * HD], F32, tag="result", name="result%d" % i)
+            half = UNITS[i] * HD // 2
+            result_i = results.tile([P, 2 * half], F32, tag="result", name="result%d" % i)
             engine.tensor_tensor(
-                out=result_i[:], in0=products[i][:, 0, :], in1=products[i][:, 1, :], op=ADD
+                out=result_i[:].rearrange("s (m r) -> s m r", r=2),
+                in0=products[i][:].rearrange("s (m r) -> s m r", r=2),
+                in1=shared[i][:].unsqueeze(2).to_broadcast([P, half, 2]),
+                op=ADD,
             )
             result[i] = result_i
 
@@ -194,7 +217,7 @@ def tile_rlaattention_pa_s_kernel(tc, x, freqs_cis, Wqkv, out_0, out_1, out_2):
                     store_unit(i)
                 else:
                     products_unit(i)
-                    if FIRST_HEAD[i] + UNITS[i] == N_ROTATED:
+                    if i < 2 or FIRST_HEAD[i] + UNITS[i] == N_ROTATED:
                         waiting = i
                     else:
                         add_unit(i, nc.gpsimd)

@@ -22,6 +22,7 @@ N_ROTATED = N_Q_HEADS + N_KV_HEADS
 UNITS = (2, 2, 2, 2, 4, 4, 2, 2, 4)
 N_UNITS = len(UNITS)
 FIRST_HEAD = [sum(UNITS[:i]) for i in range(N_UNITS)]
+VECTOR_ADDS = (0, 1, 5, 7)
 
 FLOPS = 2 * P * D * (N_Q_HEADS + 2 * N_KV_HEADS) * HD
 
@@ -39,7 +40,6 @@ def tile_rlaattention_pa_s_kernel(tc, x, freqs_cis, Wqkv, out_0, out_1, out_2):
         freqs = const.tile([P, PAIRS, 2], BF16)
         x_sb = const.tile([P, D], BF16)
         w_sb = []
-        nc.sync.dma_start(out=freqs[:], in_=freqs_cis.rearrange("s (j e) -> s j e", e=2))
         for i in range(N_UNITS):
             rows = Wqkv[FIRST_HEAD[i] * HD : (FIRST_HEAD[i] + UNITS[i]) * HD, :]
             w_i = weights.tile([P, UNITS[i] * D], BF16, tag="w", name="w%d" % i)
@@ -47,19 +47,33 @@ def tile_rlaattention_pa_s_kernel(tc, x, freqs_cis, Wqkv, out_0, out_1, out_2):
             w_sb.append(w_i)
             if i == 0:
                 nc.sync.dma_start(out=x_sb[:], in_=x.flatten_outer_dims())
+                nc.sync.dma_start(
+                    out=freqs[:], in_=freqs_cis.rearrange("s (j e) -> s j e", e=2)
+                )
 
         ident = const.tile([P, P], F32)
         make_identity(nc, ident[:])
 
         table = const.tile([P, PAIRS, 2], F32)
 
+        signed_f0 = const.tile([P, PAIRS, 2], F32)
+        signs = const.tile([P, 2], F32)
+        nc.gpsimd.memset(signs[:, 0:1], -1.0)
+        nc.gpsimd.memset(signs[:, 1:2], 1.0)
+
         def make_table():
-            nc.vector.scalar_tensor_tensor(
-                out=table[:, :, 0], in0=freqs[:, :, 0], scalar=-1.0, in1=freqs[:, :, 1],
-                op0=MULT, op1=SUBTRACT,
+            shape = [P, PAIRS, 2]
+            nc.vector.tensor_tensor(
+                out=signed_f0[:],
+                in0=freqs[:, :, 0].unsqueeze(2).to_broadcast(shape),
+                in1=signs[:].unsqueeze(1).to_broadcast(shape),
+                op=MULT,
             )
             nc.vector.tensor_tensor(
-                out=table[:, :, 1], in0=freqs[:, :, 0], in1=freqs[:, :, 1], op=SUBTRACT
+                out=table[:],
+                in0=signed_f0[:],
+                in1=freqs[:, :, 1].unsqueeze(2).to_broadcast(shape),
+                op=SUBTRACT,
             )
 
         x_codes = const.tile([P, P], U32, align_bytes=64)
@@ -195,11 +209,12 @@ def tile_rlaattention_pa_s_kernel(tc, x, freqs_cis, Wqkv, out_0, out_1, out_2):
             )
 
         with tc.manual_schedule():
-            make_table()
             transpose_unit(0)
             transpose_x()
+            quantise_unit(0)
             quantise_x()
-            transposed, quantised, waiting = 1, 0, None
+            make_table()
+            transposed, quantised, waiting = 1, 1, None
             for i in range(N_UNITS):
                 while transposed < min(i + 2 + 1, N_UNITS):
                     transpose_unit(transposed)
@@ -217,7 +232,7 @@ def tile_rlaattention_pa_s_kernel(tc, x, freqs_cis, Wqkv, out_0, out_1, out_2):
                     store_unit(i)
                 else:
                     products_unit(i)
-                    if i < 2 or FIRST_HEAD[i] + UNITS[i] == N_ROTATED:
+                    if i in VECTOR_ADDS:
                         waiting = i
                     else:
                         add_unit(i, nc.gpsimd)

@@ -19,11 +19,9 @@ PAIRS = HD // 2
 N_Q_HEADS = 16
 N_KV_HEADS = 4
 N_ROTATED = N_Q_HEADS + N_KV_HEADS
-UNITS = (2, 2, 2, 2, 4, 4, 2, 2, 4)
+UNITS = (2, 2, 2, 2, 4, 4, 4, 2, 2)
 N_UNITS = len(UNITS)
-FIRST_HEAD = [sum(UNITS[:i]) for i in range(N_UNITS)]
-VECTOR_ADDS = (0, 1, 5, 7)
-
+FIRST_HEAD = (0, 2, 4, 6, 8, 12, N_ROTATED, 16, 18)
 FLOPS = 2 * P * D * (N_Q_HEADS + 2 * N_KV_HEADS) * HD
 
 
@@ -232,8 +230,10 @@ def tile_rlaattention_pa_s_kernel(tc, x, freqs_cis, Wqkv, out_0, out_1, out_2):
                     store_unit(i)
                 else:
                     products_unit(i)
-                    if i in VECTOR_ADDS:
+                    if i < 2 or i % 3 == 2:
                         waiting = i
                     else:
                         add_unit(i, nc.gpsimd)
                         store_unit(i)
+            add_unit(waiting, nc.vector)
+            store_unit(waiting)

@@ -59,7 +59,7 @@ def tile_rlaattention_pa_s_kernel(tc, x, freqs_cis, Wqkv, out_0, out_1, out_2):
         nc.gpsimd.memset(signs[:, 0:1], -1.0)
         nc.gpsimd.memset(signs[:, 1:2], 1.0)
 
-        def make_table():
+        def make_signed_f0():
             shape = [P, PAIRS, 2]
             nc.vector.tensor_tensor(
                 out=signed_f0[:],
@@ -67,10 +67,12 @@ def tile_rlaattention_pa_s_kernel(tc, x, freqs_cis, Wqkv, out_0, out_1, out_2):
                 in1=signs[:].unsqueeze(1).to_broadcast(shape),
                 op=MULT,
             )
+
+        def make_table():
             nc.vector.tensor_tensor(
                 out=table[:],
                 in0=signed_f0[:],
-                in1=freqs[:, :, 1].unsqueeze(2).to_broadcast(shape),
+                in1=freqs[:, :, 1].unsqueeze(2).to_broadcast([P, PAIRS, 2]),
                 op=SUBTRACT,
             )
 
@@ -83,6 +85,9 @@ def tile_rlaattention_pa_s_kernel(tc, x, freqs_cis, Wqkv, out_0, out_1, out_2):
             bank = flipped.tile([P, 2, P], F32, tag="bank", name="x_bank")
             for u in range(2):
                 nc.tensor.transpose(bank[:, u, :], x_words[:, u * P : (u + 1) * P], ident[:])
+            return bank
+
+        def copy_x(bank):
             nc.vector.tensor_copy(
                 out=x_grouped[:].bitcast(F32).rearrange("q (s u) -> q s u", u=2),
                 in_=bank[:].rearrange("q u s -> q s u"),
@@ -194,7 +199,7 @@ def tile_rlaattention_pa_s_kernel(tc, x, freqs_cis, Wqkv, out_0, out_1, out_2):
             )
             result[i] = result_i
 
-        def store_unit(i):
+        def store_unit(i, queue):
             first = FIRST_HEAD[i]
             if first < N_Q_HEADS:
                 heads = head_views[0][:, first : first + UNITS[i], :]
@@ -202,38 +207,46 @@ def tile_rlaattention_pa_s_kernel(tc, x, freqs_cis, Wqkv, out_0, out_1, out_2):
                 heads = head_views[1][:, first - N_Q_HEADS : first - N_Q_HEADS + UNITS[i], :]
             else:
                 heads = head_views[2][:, first - N_ROTATED : first - N_ROTATED + UNITS[i], :]
-            nc.sync.dma_start(
+            queue.dma_start(
                 out=heads, in_=result[i][:].rearrange("s (h f) -> s h f", h=UNITS[i])
             )
 
         with tc.manual_schedule():
             transpose_unit(0)
-            transpose_x()
-            quantise_unit(0)
-            quantise_x()
+            x_bank = transpose_x()
+            make_signed_f0()
+            copy_x(x_bank)
             make_table()
-            transposed, quantised, waiting = 1, 1, None
+            quantise_x()
+            quantise_unit(0)
+            transposed, quantised, waiting = 1, 1, []
             for i in range(N_UNITS):
                 while transposed < min(i + 2 + 1, N_UNITS):
                     transpose_unit(transposed)
                     transposed += 1
-                while quantised < min(i + 1 + 1, N_UNITS):
+                ahead = 1 if i < N_UNITS - 3 else 2
+                last_quantise = quantised == N_UNITS
+                while quantised < min(i + ahead + 1, N_UNITS):
                     quantise_unit(quantised)
                     quantised += 1
                 multiply_unit(i)
-                if waiting is not None:
-                    add_unit(waiting, nc.vector)
-                    store_unit(waiting)
-                    waiting = None
                 if FIRST_HEAD[i] >= N_ROTATED:
                     copy_values(i)
-                    store_unit(i)
-                else:
+                    store_unit(i, nc.scalar)
+                elif last_quantise:
                     products_unit(i)
-                    if i < 2 or i % 3 == 2:
-                        waiting = i
-                    else:
+                while waiting:
+                    add_unit(waiting[0], nc.vector)
+                    store_unit(waiting[0], nc.sync)
+                    waiting.remove(waiting[0])
+                if FIRST_HEAD[i] < N_ROTATED:
+                    if not last_quantise:
+                        products_unit(i)
+                    if i in (3, 4):
                         add_unit(i, nc.gpsimd)
-                        store_unit(i)
-            add_unit(waiting, nc.vector)
-            store_unit(waiting)
+                        store_unit(i, nc.sync)
+                    else:
+                        waiting.append(i)
+            for i in waiting:
+                add_unit(i, nc.vector)
+                store_unit(i, nc.sync)

@@ -180,16 +180,16 @@ def tile_rlaattention_pa_s_kernel(tc, x, freqs_cis, Wqkv, out_0, out_1, out_2):
             )
             shared[i] = shared_i
 
-        def add_unit(i, engine):
-            half = UNITS[i] * HD // 2
-            result_i = results.tile([P, 2 * half], F32, tag="result", name="result%d" % i)
+        def add_heads(i, first, last, engine):
+            if i not in result:
+                result[i] = results.tile([P, UNITS[i] * HD], F32, tag="result", name="result%d" % i)
+            lo, hi = first * HD, last * HD
             engine.tensor_tensor(
-                out=result_i[:].rearrange("s (m r) -> s m r", r=2),
-                in0=products[i][:].rearrange("s (m r) -> s m r", r=2),
-                in1=shared[i][:].unsqueeze(2).to_broadcast([P, half, 2]),
+                out=result[i][:, lo:hi].rearrange("s (m r) -> s m r", r=2),
+                in0=products[i][:, lo:hi].rearrange("s (m r) -> s m r", r=2),
+                in1=shared[i][:, lo // 2 : hi // 2].unsqueeze(2).to_broadcast([P, (hi - lo) // 2, 2]),
                 op=ADD,
             )
-            result[i] = result_i
 
         def copy_values(i):
             result_i = results.tile([P, UNITS[i] * HD], F32, tag="result", name="result%d" % i)
@@ -199,17 +199,25 @@ def tile_rlaattention_pa_s_kernel(tc, x, freqs_cis, Wqkv, out_0, out_1, out_2):
             )
             result[i] = result_i
 
-        def store_unit(i, queue):
-            first = FIRST_HEAD[i]
-            if first < N_Q_HEADS:
-                heads = head_views[0][:, first : first + UNITS[i], :]
-            elif first < N_ROTATED:
-                heads = head_views[1][:, first - N_Q_HEADS : first - N_Q_HEADS + UNITS[i], :]
+        def store_heads(i, first, last, queue):
+            head = FIRST_HEAD[i] + first
+            n = last - first
+            if head < N_Q_HEADS:
+                heads = head_views[0][:, head : head + n, :]
+            elif head < N_ROTATED:
+                heads = head_views[1][:, head - N_Q_HEADS : head - N_Q_HEADS + n, :]
             else:
-                heads = head_views[2][:, first - N_ROTATED : first - N_ROTATED + UNITS[i], :]
+                heads = head_views[2][:, head - N_ROTATED : head - N_ROTATED + n, :]
             queue.dma_start(
-                out=heads, in_=result[i][:].rearrange("s (h f) -> s h f", h=UNITS[i])
+                out=heads,
+                in_=result[i][:, first * HD : last * HD].rearrange("s (h f) -> s h f", h=n),
             )
+
+        by_gpsimd = {3: 2, 4: 2}
+
+        def add_and_store(i, first, last, engine):
+            add_heads(i, first, last, engine)
+            store_heads(i, first, last, nc.sync)
 
         with tc.manual_schedule():
             transpose_unit(0)
@@ -232,21 +240,18 @@ def tile_rlaattention_pa_s_kernel(tc, x, freqs_cis, Wqkv, out_0, out_1, out_2):
                 multiply_unit(i)
                 if FIRST_HEAD[i] >= N_ROTATED:
                     copy_values(i)
-                    store_unit(i, nc.scalar)
+                    store_heads(i, 0, UNITS[i], nc.scalar)
                 elif last_quantise:
                     products_unit(i)
-                while waiting:
-                    add_unit(waiting[0], nc.vector)
-                    store_unit(waiting[0], nc.sync)
-                    waiting.remove(waiting[0])
+                for j in [j for j in waiting if j + (2 if j in by_gpsimd else 1) <= i]:
+                    add_and_store(j, by_gpsimd.get(j, 0), UNITS[j], nc.vector)
+                    waiting.remove(j)
                 if FIRST_HEAD[i] < N_ROTATED:
                     if not last_quantise:
                         products_unit(i)
-                    if i in (3, 4):
-                        add_unit(i, nc.gpsimd)
-                        store_unit(i, nc.sync)
-                    else:
+                    if i in by_gpsimd:
+                        add_and_store(i, 0, by_gpsimd[i], nc.gpsimd)
+                    if by_gpsimd.get(i, 0) < UNITS[i]:
                         waiting.append(i)
-            for i in waiting:
-                add_unit(i, nc.vector)
-                store_unit(i, nc.sync)
+            for j in waiting:
+                add_and_store(j, 0, UNITS[j], nc.vector)

@@ -32,8 +32,9 @@ def tile_rlaattention_pa_s_kernel(tc, x, freqs_cis, Wqkv, out_0, out_1, out_2):
         weights = ctx.enter_context(tc.tile_pool(name="weights", bufs=N_UNITS))
         stage = ctx.enter_context(tc.tile_pool(name="stage", bufs=4))
         results = ctx.enter_context(tc.tile_pool(name="results", bufs=N_UNITS))
-        flipped = ctx.enter_context(tc.psum_pool(name="flipped", bufs=4))
+        flipped = ctx.enter_context(tc.psum_pool(name="flipped", bufs=3))
         sums = ctx.enter_context(tc.psum_pool(name="sums", bufs=2))
+        unread_sums = ctx.enter_context(tc.psum_pool(name="unread_sums", bufs=1))
 
         freqs = const.tile([P, PAIRS, 2], BF16)
         x_sb = const.tile([P, D], BF16)
@@ -97,6 +98,25 @@ def tile_rlaattention_pa_s_kernel(tc, x, freqs_cis, Wqkv, out_0, out_1, out_2):
             nc.vector.quantize_mx(
                 out=x_codes[:].bitcast(FP8X4), scales=x_scales[:], in_=x_grouped[:]
             )
+
+        zeros = const.tile([P, 4 * P], BF16, align_bytes=64)
+        zero_codes = const.tile([P, P], U32, align_bytes=64)
+        zero_scales = const.tile([P, P], U8, align_bytes=64)
+        unread = unread_sums.tile([P, P], F32, name="unread")
+        nc.vector.memset(zeros[:], 0.0)
+        nc.vector.quantize_mx(out=zero_codes[:].bitcast(FP8X4), scales=zero_scales[:], in_=zeros[:])
+
+        def multiply_zeros(n):
+            for k in range(n):
+                nc.tensor.matmul_mx(
+                    out=unread[:],
+                    lhsT=zero_codes[:].bitcast(FP8X4),
+                    lhsT_scale=zero_scales[:],
+                    rhs=zero_codes[:].bitcast(FP8X4),
+                    rhs_scale=zero_scales[:],
+                    start=True,
+                    stop=True,
+                )
 
         head_views = [out.rearrange("b h s f -> s (b h) f") for out in (out_0, out_1, out_2)]
         grouped, codes, scales, acc, both = {}, {}, {}, {}, {}
@@ -220,8 +240,10 @@ def tile_rlaattention_pa_s_kernel(tc, x, freqs_cis, Wqkv, out_0, out_1, out_2):
             store_heads(i, first, last, nc.sync)
 
         with tc.manual_schedule():
+            multiply_zeros(12)
             transpose_unit(0)
             x_bank = transpose_x()
+            multiply_zeros(4)
             make_signed_f0()
             copy_x(x_bank)
             make_table()
@@ -231,6 +253,8 @@ def tile_rlaattention_pa_s_kernel(tc, x, freqs_cis, Wqkv, out_0, out_1, out_2):
             for i in range(N_UNITS):
                 while transposed < min(i + 2 + 1, N_UNITS):
                     transpose_unit(transposed)
+                    if transposed < 3:
+                        multiply_zeros(4)
                     transposed += 1
                 ahead = 1 if i < N_UNITS - 3 else 2
                 last_quantise = quantised == N_UNITS

@@ -103,7 +103,7 @@ def tile_rlaattention_pa_s_kernel(tc, x, freqs_cis, Wqkv, out_0, out_1, out_2):
         zero_codes = const.tile([P, P], U32, align_bytes=64)
         zero_scales = const.tile([P, P], U8, align_bytes=64)
         unread = unread_sums.tile([P, P], F32, name="unread")
-        nc.vector.memset(zeros[:], 0.0)
+        nc.vector.memset(zeros[:].bitcast(F32), 0.0)
         nc.vector.quantize_mx(out=zero_codes[:].bitcast(FP8X4), scales=zero_scales[:], in_=zeros[:])
 
         def multiply_zeros(n):
@@ -254,10 +254,9 @@ def tile_rlaattention_pa_s_kernel(tc, x, freqs_cis, Wqkv, out_0, out_1, out_2):
                 while transposed < min(i + 2 + 1, N_UNITS):
                     transpose_unit(transposed)
                     if transposed < 3:
-                        multiply_zeros(4)
+                        multiply_zeros(5 - transposed)
                     transposed += 1
                 ahead = 1 if i < N_UNITS - 3 else 2
-                last_quantise = quantised == N_UNITS
                 while quantised < min(i + ahead + 1, N_UNITS):
                     quantise_unit(quantised)
                     quantised += 1
@@ -265,17 +264,15 @@ def tile_rlaattention_pa_s_kernel(tc, x, freqs_cis, Wqkv, out_0, out_1, out_2):
                 if FIRST_HEAD[i] >= N_ROTATED:
                     copy_values(i)
                     store_heads(i, 0, UNITS[i], nc.scalar)
-                elif last_quantise:
+                else:
                     products_unit(i)
-                for j in [j for j in waiting if j + (2 if j in by_gpsimd else 1) <= i]:
-                    add_and_store(j, by_gpsimd.get(j, 0), UNITS[j], nc.vector)
-                    waiting.remove(j)
-                if FIRST_HEAD[i] < N_ROTATED:
-                    if not last_quantise:
-                        products_unit(i)
-                    if i in by_gpsimd:
-                        add_and_store(i, 0, by_gpsimd[i], nc.gpsimd)
-                    if by_gpsimd.get(i, 0) < UNITS[i]:
-                        waiting.append(i)
+                if i in by_gpsimd:
+                    add_and_store(i, 0, by_gpsimd[i], nc.gpsimd)
+                else:
+                    for j in [j for j in waiting if j + (2 if j in by_gpsimd else 1) <= i]:
+                        add_and_store(j, by_gpsimd.get(j, 0), UNITS[j], nc.vector)
+                        waiting.remove(j)
+                if FIRST_HEAD[i] < N_ROTATED and by_gpsimd.get(i, 0) < UNITS[i]:
+                    waiting.append(i)
             for j in waiting:
                 add_and_store(j, 0, UNITS[j], nc.vector)

@@ -46,6 +46,7 @@ def tile_rlaattention_pa_s_kernel(tc, x, freqs_cis, Wqkv, out_0, out_1, out_2):
             w_sb.append(w_i)
             if i == 0:
                 nc.sync.dma_start(out=x_sb[:], in_=x.flatten_outer_dims())
+            if i == 1:
                 nc.sync.dma_start(
                     out=freqs[:], in_=freqs_cis.rearrange("s (j e) -> s j e", e=2)
                 )
@@ -244,17 +245,17 @@ def tile_rlaattention_pa_s_kernel(tc, x, freqs_cis, Wqkv, out_0, out_1, out_2):
             transpose_unit(0)
             x_bank = transpose_x()
             multiply_zeros(4)
-            make_signed_f0()
             copy_x(x_bank)
-            make_table()
             quantise_x()
             quantise_unit(0)
+            make_signed_f0()
+            make_table()
             transposed, quantised, waiting = 1, 1, []
             for i in range(N_UNITS):
                 while transposed < min(i + 2 + 1, N_UNITS):
                     transpose_unit(transposed)
-                    if transposed < 3:
-                        multiply_zeros(5 - transposed)
+                    if transposed == 1:
+                        multiply_zeros(4)
                     transposed += 1
                 ahead = 1 if i < N_UNITS - 3 else 2
                 while quantised < min(i + ahead + 1, N_UNITS):

@@ -256,6 +256,8 @@ def tile_rlaattention_pa_s_kernel(tc, x, freqs_cis, Wqkv, out_0, out_1, out_2):
                     transpose_unit(transposed)
                     if transposed == 1:
                         multiply_zeros(4)
+                    elif UNITS[transposed] == 4 and transposed < 6:
+                        multiply_zeros(2)
                     transposed += 1
                 ahead = 1 if i < N_UNITS - 3 else 2
                 while quantised < min(i + ahead + 1, N_UNITS):

from contextlib import ExitStack

import concourse.mybir as mybir
from concourse.masks import make_identity

BF16 = mybir.dt.bfloat16
F32 = mybir.dt.float32
U32 = mybir.dt.uint32
U8 = mybir.dt.uint8
FP8X4 = mybir.dt.float8_e4m3fn_x4
MULT = mybir.AluOpType.mult
ADD = mybir.AluOpType.add
SUBTRACT = mybir.AluOpType.subtract

P = 128
D = 512
HD = 128
PAIRS = HD // 2
N_Q_HEADS = 16
N_KV_HEADS = 4
N_ROTATED = N_Q_HEADS + N_KV_HEADS
UNITS = (2, 2, 2, 2, 4, 4, 4, 2, 2)
N_UNITS = len(UNITS)
FIRST_HEAD = (0, 2, 4, 6, 8, 12, N_ROTATED, 16, 18)
FLOPS = 2 * P * D * (N_Q_HEADS + 2 * N_KV_HEADS) * HD


def tile_rlaattention_pa_s_kernel(tc, x, freqs_cis, Wqkv, out_0, out_1, out_2):
    nc = tc.nc
    with ExitStack() as ctx:
        const = ctx.enter_context(tc.tile_pool(name="const", bufs=1))
        weights = ctx.enter_context(tc.tile_pool(name="weights", bufs=N_UNITS))
        stage = ctx.enter_context(tc.tile_pool(name="stage", bufs=4))
        results = ctx.enter_context(tc.tile_pool(name="results", bufs=N_UNITS))
        flipped = ctx.enter_context(tc.psum_pool(name="flipped", bufs=3))
        sums = ctx.enter_context(tc.psum_pool(name="sums", bufs=2))
        unread_sums = ctx.enter_context(tc.psum_pool(name="unread_sums", bufs=1))

        freqs = const.tile([P, PAIRS, 2], BF16)
        x_sb = const.tile([P, D], BF16)
        w_sb = []
        for i in range(N_UNITS):
            rows = Wqkv[FIRST_HEAD[i] * HD : (FIRST_HEAD[i] + UNITS[i]) * HD, :]
            w_i = weights.tile([P, UNITS[i] * D], BF16, tag="w", name="w%d" % i)
            nc.sync.dma_start(out=w_i[:], in_=rows.rearrange("(p b) k -> p (b k)", p=P))
            w_sb.append(w_i)
            if i == 0:
                nc.sync.dma_start(out=x_sb[:], in_=x.flatten_outer_dims())
            if i == 1:
                nc.sync.dma_start(
                    out=freqs[:], in_=freqs_cis.rearrange("s (j e) -> s j e", e=2)
                )

        ident = const.tile([P, P], F32)
        make_identity(nc, ident[:])

        table = const.tile([P, PAIRS, 2], F32)

        signed_f0 = const.tile([P, PAIRS, 2], F32)
        signs = const.tile([P, 2], F32)
        nc.gpsimd.memset(signs[:, 0:1], -1.0)
        nc.gpsimd.memset(signs[:, 1:2], 1.0)

        def make_signed_f0():
            shape = [P, PAIRS, 2]
            nc.vector.tensor_tensor(
                out=signed_f0[:],
                in0=freqs[:, :, 0].unsqueeze(2).to_broadcast(shape),
                in1=signs[:].unsqueeze(1).to_broadcast(shape),
                op=MULT,
            )

        def make_table():
            nc.vector.tensor_tensor(
                out=table[:],
                in0=signed_f0[:],
                in1=freqs[:, :, 1].unsqueeze(2).to_broadcast([P, PAIRS, 2]),
                op=SUBTRACT,
            )

        x_codes = const.tile([P, P], U32, align_bytes=64)
        x_scales = const.tile([P, P], U8, align_bytes=64)
        x_grouped = const.tile([P, 4 * P], BF16, align_bytes=64)

        def transpose_x():
            x_words = x_sb[:].bitcast(F32)
            bank = flipped.tile([P, 2, P], F32, tag="bank", name="x_bank")
            for u in range(2):
                nc.tensor.transpose(bank[:, u, :], x_words[:, u * P : (u + 1) * P], ident[:])
            return bank

        def copy_x(bank):
            nc.vector.tensor_copy(
                out=x_grouped[:].bitcast(F32).rearrange("q (s u) -> q s u", u=2),
                in_=bank[:].rearrange("q u s -> q s u"),
            )

        def quantise_x():
            nc.vector.quantize_mx(
                out=x_codes[:].bitcast(FP8X4), scales=x_scales[:], in_=x_grouped[:]
            )

        zeros = const.tile([P, 4 * P], BF16, align_bytes=64)
        zero_codes = const.tile([P, P], U32, align_bytes=64)
        zero_scales = const.tile([P, P], U8, align_bytes=64)
        unread = unread_sums.tile([P, P], F32, name="unread")
        nc.vector.memset(zeros[:].bitcast(F32), 0.0)
        nc.vector.quantize_mx(out=zero_codes[:].bitcast(FP8X4), scales=zero_scales[:], in_=zeros[:])

        def multiply_zeros(n):
            for k in range(n):
                nc.tensor.matmul_mx(
                    out=unread[:],
                    lhsT=zero_codes[:].bitcast(FP8X4),
                    lhsT_scale=zero_scales[:],
                    rhs=zero_codes[:].bitcast(FP8X4),
                    rhs_scale=zero_scales[:],
                    start=True,
                    stop=True,
                )

        head_views = [out.rearrange("b h s f -> s (b h) f") for out in (out_0, out_1, out_2)]
        grouped, codes, scales, acc, both = {}, {}, {}, {}, {}
        products, shared, result = {}, {}, {}

        def transpose_unit(i):
            per_slot = UNITS[i] // 2
            w_words = w_sb[i][:].bitcast(F32)
            grouped_i = stage.tile(
                [P, 4 * UNITS[i] * HD], BF16, align_bytes=64, tag="grouped", name="grouped%d" % i
            )
            grouped[i] = grouped_i
            words = grouped_i[:].bitcast(F32).rearrange("q (e p w) -> q e p w", e=2, p=P)
            for e0 in range(0, 2, 2 // per_slot):
                slots = range(e0, e0 + 2 // per_slot)
                bank = flipped.tile(
                    [P, len(slots), per_slot, 2, P], F32, tag="bank", name="bank%d_%d" % (i, e0)
                )
                for e in slots:
                    for b in range(per_slot):
                        row = 2 * b + (1 - e if FIRST_HEAD[i] < N_ROTATED else e)
                        for u in range(2):
                            word = (row * 2 + u) * P
                            nc.tensor.transpose(
                                bank[:, e - e0, b, u, :], w_words[:, word : word + P], ident[:]
                            )
                nc.scalar.copy(
                    out=words[:, e0 : e0 + len(slots), :, :],
                    in_=bank[:].rearrange("q e b u p -> q e p (b u)"),
                )

        def quantise_unit(i):
            width = UNITS[i] * HD
            codes_i = stage.tile([P, width], U32, align_bytes=64, tag="codes", name="codes%d" % i)
            scales_i = stage.tile([P, width], U8, align_bytes=64, tag="scales", name="scales%d" % i)
            nc.vector.quantize_mx(
                out=codes_i[:].bitcast(FP8X4), scales=scales_i[:], in_=grouped[i][:]
            )
            codes[i], scales[i] = codes_i, scales_i

        def multiply_unit(i):
            half = UNITS[i] * HD // 2

            def multiply(out, first, last, start, stop):
                nc.tensor.matmul_mx(
                    out=out,
                    lhsT=x_codes[:].bitcast(FP8X4),
                    lhsT_scale=x_scales[:],
                    rhs=codes[i][:, first:last].bitcast(FP8X4),
                    rhs_scale=scales[i][:, first:last],
                    start=start,
                    stop=stop,
                )

            acc_i = sums.tile([P, 2 * half], F32, tag="acc", name="acc%d" % i)
            multiply(acc_i[:], 0, 2 * half, True, True)
            acc[i] = acc_i
            if FIRST_HEAD[i] < N_ROTATED:
                both_i = sums.tile([P, half], F32, tag="both", name="both%d" % i)
                multiply(both_i[:], 0, half, True, False)
                multiply(both_i[:], half, 2 * half, False, True)
                both[i] = both_i

        def products_unit(i):
            n_heads = UNITS[i]
            half = n_heads * HD // 2
            products_i = stage.tile([P, 2 * half], F32, tag="products", name="products%d" % i)
            nc.vector.tensor_tensor(
                out=products_i[:].rearrange("s (h j r) -> s h j r", h=n_heads, r=2),
                in0=acc[i][:].rearrange("s (r h j) -> s h j r", r=2, h=n_heads),
                in1=table[:].unsqueeze(1).to_broadcast([P, n_heads, PAIRS, 2]),
                op=MULT,
            )
            products[i] = products_i
            shared_i = stage.tile([P, half], F32, tag="shared", name="shared%d" % i)
            nc.vector.tensor_tensor(
                out=shared_i[:].rearrange("s (h j) -> s h j", h=n_heads),
                in0=both[i][:].rearrange("s (h j) -> s h j", h=n_heads),
                in1=freqs[:, :, 1].unsqueeze(1).to_broadcast([P, n_heads, PAIRS]),
                op=MULT,
            )
            shared[i] = shared_i

        def add_heads(i, first, last, engine):
            if i not in result:
                result[i] = results.tile([P, UNITS[i] * HD], F32, tag="result", name="result%d" % i)
            lo, hi = first * HD, last * HD
            engine.tensor_tensor(
                out=result[i][:, lo:hi].rearrange("s (m r) -> s m r", r=2),
                in0=products[i][:, lo:hi].rearrange("s (m r) -> s m r", r=2),
                in1=shared[i][:, lo // 2 : hi // 2].unsqueeze(2).to_broadcast([P, (hi - lo) // 2, 2]),
                op=ADD,
            )

        def copy_values(i):
            result_i = results.tile([P, UNITS[i] * HD], F32, tag="result", name="result%d" % i)
            nc.scalar.copy(
                out=result_i[:].rearrange("s (m e) -> s m e", e=2),
                in_=acc[i][:].rearrange("s (e m) -> s m e", e=2),
            )
            result[i] = result_i

        def store_heads(i, first, last, queue):
            head = FIRST_HEAD[i] + first
            n = last - first
            if head < N_Q_HEADS:
                heads = head_views[0][:, head : head + n, :]
            elif head < N_ROTATED:
                heads = head_views[1][:, head - N_Q_HEADS : head - N_Q_HEADS + n, :]
            else:
                heads = head_views[2][:, head - N_ROTATED : head - N_ROTATED + n, :]
            queue.dma_start(
                out=heads,
                in_=result[i][:, first * HD : last * HD].rearrange("s (h f) -> s h f", h=n),
            )

        by_gpsimd = {3: 2, 4: 2}

        def add_and_store(i, first, last, engine):
            add_heads(i, first, last, engine)
            store_heads(i, first, last, nc.sync)

        with tc.manual_schedule():
            multiply_zeros(12)
            transpose_unit(0)
            x_bank = transpose_x()
            multiply_zeros(4)
            copy_x(x_bank)
            quantise_x()
            quantise_unit(0)
            make_signed_f0()
            make_table()
            transposed, quantised, waiting = 1, 1, []
            for i in range(N_UNITS):
                while transposed < min(i + 2 + 1, N_UNITS):
                    transpose_unit(transposed)
                    if transposed == 1:
                        multiply_zeros(4)
                    elif UNITS[transposed] == 4 and transposed < 6:
                        multiply_zeros(2)
                    transposed += 1
                ahead = 1 if i < N_UNITS - 3 else 2
                while quantised < min(i + ahead + 1, N_UNITS):
                    quantise_unit(quantised)
                    quantised += 1
                multiply_unit(i)
                if FIRST_HEAD[i] >= N_ROTATED:
                    copy_values(i)
                    store_heads(i, 0, UNITS[i], nc.scalar)
                else:
                    products_unit(i)
                if i in by_gpsimd:
                    add_and_store(i, 0, by_gpsimd[i], nc.gpsimd)
                else:
                    for j in [j for j in waiting if j + (2 if j in by_gpsimd else 1) <= i]:
                        add_and_store(j, by_gpsimd.get(j, 0), UNITS[j], nc.vector)
                        waiting.remove(j)
                if FIRST_HEAD[i] < N_ROTATED and by_gpsimd.get(i, 0) < UNITS[i]:
                    waiting.append(i)
            for j in waiting:
                add_and_store(j, 0, UNITS[j], nc.vector)
